import numpy as np
import ml_dtypes

BF16 = ml_dtypes.bfloat16


def bf(x):
    return np.asarray(x, np.float32).astype(BF16)


def f32(x):
    return np.asarray(x, np.float32)


def f64(x):
    return np.asarray(x).astype(np.float64)


def striped(idx):
    return np.tile(idx.reshape(-1, 16).T, (8, 1))


D, M, S, N, NA, R = 128, 128, 1024, 1024, 4, 32
L = N // NA


def setup_inputs():
    return {"table": bf(np.random.standard_normal((D, S))), "w": bf(np.random.standard_normal((D, M)) / np.sqrt(D)), "wa": bf(np.random.standard_normal((D, NA * R)) / np.sqrt(D)), "wb": bf(0.5 * np.random.standard_normal((NA * R, M)) / np.sqrt(R)), "offs": striped(np.random.permutation(np.tile(np.arange(S), 2))[:N])}


def reference(table, w, wa, wb, offs):
    idx = offs[:16].T.reshape(-1)
    x = f64(table)[:, idx]
    u = f64(wa).T @ x
    own = (np.arange(NA * R)[:, None] // R) == (np.arange(N)[None, :] // L)
    return f64(w).T @ x + f64(wb).T @ (u * own)

@@ -1,0 +1,62 @@
+import concourse.mybir as mybir
+
+BF16, F32, U16 = mybir.dt.bfloat16, mybir.dt.float32, mybir.dt.uint16
+
+D = 128
+M = 128
+S = 1024
+N = 1024
+NA = 4
+R = 32
+L = N // NA
+K = L // 16
+
+FLOPS = 2 * D * M * N + 2 * D * (NA * R) * N + 2 * R * M * N
+
+
+def tile_llamaattentionwithlora_kernel(tc, table, w, wa, wb, offs, out):
+    nc = tc.nc
+    with (
+        tc.tile_pool(name="held", bufs=1) as held,
+        tc.tile_pool(name="staged", bufs=NA) as staged,
+        tc.psum_pool(name="down", bufs=NA) as down,
+        tc.psum_pool(name="proj", bufs=NA) as proj,
+    ):
+        offsets = held.tile([128, N // 16], U16, name="offsets")
+        nc.sync.dma_start(offsets[:], offs)
+        table_sb = held.tile([D, S], BF16, name="table_sb")
+        nc.scalar.dma_start(table_sb[:], table)
+        wa_sb = held.tile([D, NA * R], BF16, name="wa_sb")
+        nc.sync.dma_start(wa_sb[:], wa)
+        w_sb = held.tile([D, M], BF16, name="w_sb")
+        nc.scalar.dma_start(w_sb[:], w)
+        wb_sb = held.tile([NA * R, M], BF16, name="wb_sb")
+        nc.sync.dma_start(wb_sb[:], wb)
+
+        u_own = held.tile([NA * R, N], BF16, name="u_own")
+        nc.vector.memset(u_own[:], 0.0)
+
+        for a in range(NA):
+            picked = table_sb[:].indirect(offsets[:, a * K : (a + 1) * K])
+            u_ps = down.tile([NA * R, L], F32, name="u_ps")
+            nc.tensor.matmul(u_ps[:], wa_sb[:], picked, start=True, stop=True)
+            own_rows = slice(a * R, (a + 1) * R)
+            if a % 2 == 0:
+                nc.vector.tensor_copy(u_own[own_rows, a * L : (a + 1) * L], u_ps[own_rows, :])
+            else:
+                nc.scalar.copy(u_own[own_rows, a * L : (a + 1) * L], u_ps[own_rows, :])
+
+        out_ps = [proj.tile([M, L], F32, name="out_ps") for a in range(NA)]
+        for a in range(NA):
+            picked = table_sb[:].indirect(offsets[:, a * K : (a + 1) * K])
+            nc.tensor.matmul(out_ps[a][:], w_sb[:], picked, start=True, stop=False)
+
+        for a in range(NA):
+            nc.tensor.matmul(out_ps[a][:], wb_sb[:], u_own[:, a * L : (a + 1) * L], start=False, stop=True)
+            out_sb = staged.tile([M, L], F32, name="out_sb")
+            if a % 2 == 0:
+                nc.vector.tensor_copy(out_sb[:], out_ps[a][:])
+                nc.sync.dma_start(out[:, a * L : (a + 1) * L], out_sb[:])
+            else:
+                nc.scalar.copy(out_sb[:], out_ps[a][:])
+                nc.scalar.dma_start(out[:, a * L : (a + 1) * L], out_sb[:])

@@ -9,7 +9,9 @@ N = 1024
 NA = 4
 R = 32
 L = N // NA
-K = L // 16
+PIECE = 512
+NP = N // PIECE
+K = PIECE // 16
 
 FLOPS = 2 * D * M * N + 2 * D * (NA * R) * N + 2 * R * M * N
 
@@ -18,9 +20,9 @@ def tile_llamaattentionwithlora_kernel(tc, table, w, wa, wb, offs, out):
     nc = tc.nc
     with (
         tc.tile_pool(name="held", bufs=1) as held,
-        tc.tile_pool(name="staged", bufs=NA) as staged,
-        tc.psum_pool(name="down", bufs=NA) as down,
-        tc.psum_pool(name="proj", bufs=NA) as proj,
+        tc.tile_pool(name="staged", bufs=NP) as staged,
+        tc.psum_pool(name="down", bufs=NP) as down,
+        tc.psum_pool(name="proj", bufs=NP) as proj,
     ):
         offsets = held.tile([128, N // 16], U16, name="offsets")
         nc.sync.dma_start(offsets[:], offs)
@@ -36,27 +38,28 @@ def tile_llamaattentionwithlora_kernel(tc, table, w, wa, wb, offs, out):
         u_own = held.tile([NA * R, N], BF16, name="u_own")
         nc.vector.memset(u_own[:], 0.0)
 
-        for a in range(NA):
-            picked = table_sb[:].indirect(offsets[:, a * K : (a + 1) * K])
-            u_ps = down.tile([NA * R, L], F32, name="u_ps")
+        for p in range(NP):
+            picked = table_sb[:].indirect(offsets[:, p * K : (p + 1) * K])
+            u_ps = down.tile([NA * R, PIECE], F32, name="u_ps")
             nc.tensor.matmul(u_ps[:], wa_sb[:], picked, start=True, stop=True)
-            own_rows = slice(a * R, (a + 1) * R)
-            if a % 2 == 0:
-                nc.vector.tensor_copy(u_own[own_rows, a * L : (a + 1) * L], u_ps[own_rows, :])
-            else:
-                nc.scalar.copy(u_own[own_rows, a * L : (a + 1) * L], u_ps[own_rows, :])
+            for a in range(p * PIECE // L, (p + 1) * PIECE // L):
+                own_rows = slice(a * R, (a + 1) * R)
+                if a % 2 == 0:
+                    nc.vector.tensor_copy(u_own[own_rows, a * L : (a + 1) * L], u_ps[own_rows, a * L - p * PIECE : (a + 1) * L - p * PIECE])
+                else:
+                    nc.scalar.copy(u_own[own_rows, a * L : (a + 1) * L], u_ps[own_rows, a * L - p * PIECE : (a + 1) * L - p * PIECE])
 
-        out_ps = [proj.tile([M, L], F32, name="out_ps") for a in range(NA)]
-        for a in range(NA):
-            picked = table_sb[:].indirect(offsets[:, a * K : (a + 1) * K])
-            nc.tensor.matmul(out_ps[a][:], w_sb[:], picked, start=True, stop=False)
+        out_ps = [proj.tile([M, PIECE], F32, name="out_ps") for p in range(NP)]
+        for p in range(NP):
+            picked = table_sb[:].indirect(offsets[:, p * K : (p + 1) * K])
+            nc.tensor.matmul(out_ps[p][:], w_sb[:], picked, start=True, stop=False)
 
-        for a in range(NA):
-            nc.tensor.matmul(out_ps[a][:], wb_sb[:], u_own[:, a * L : (a + 1) * L], start=False, stop=True)
-            out_sb = staged.tile([M, L], F32, name="out_sb")
-            if a % 2 == 0:
-                nc.vector.tensor_copy(out_sb[:], out_ps[a][:])
-                nc.sync.dma_start(out[:, a * L : (a + 1) * L], out_sb[:])
+        for p in range(NP):
+            nc.tensor.matmul(out_ps[p][:], wb_sb[:], u_own[:, p * PIECE : (p + 1) * PIECE], start=False, stop=True)
+            out_sb = staged.tile([M, PIECE], F32, name="out_sb")
+            if p % 2 == 0:
+                nc.vector.tensor_copy(out_sb[:], out_ps[p][:])
+                nc.sync.dma_start(out[:, p * PIECE : (p + 1) * PIECE], out_sb[:])
             else:
-                nc.scalar.copy(out_sb[:], out_ps[a][:])
-                nc.scalar.dma_start(out[:, a * L : (a + 1) * L], out_sb[:])
+                nc.scalar.copy(out_sb[:], out_ps[p][:])
+                nc.scalar.dma_start(out[:, p * PIECE : (p + 1) * PIECE], out_sb[:])

@@ -24,16 +24,16 @@ def tile_llamaattentionwithlora_kernel(tc, table, w, wa, wb, offs, out):
         tc.psum_pool(name="down", bufs=NP) as down,
         tc.psum_pool(name="proj", bufs=NP) as proj,
     ):
+        table_sb = held.tile([D, S], BF16, name="table_sb")
+        nc.sync.dma_start(table_sb[:], table)
         offsets = held.tile([128, N // 16], U16, name="offsets")
         nc.sync.dma_start(offsets[:], offs)
-        table_sb = held.tile([D, S], BF16, name="table_sb")
-        nc.scalar.dma_start(table_sb[:], table)
         wa_sb = held.tile([D, NA * R], BF16, name="wa_sb")
-        nc.sync.dma_start(wa_sb[:], wa)
+        nc.scalar.dma_start(wa_sb[:], wa)
         w_sb = held.tile([D, M], BF16, name="w_sb")
         nc.scalar.dma_start(w_sb[:], w)
         wb_sb = held.tile([NA * R, M], BF16, name="wb_sb")
-        nc.sync.dma_start(wb_sb[:], wb)
+        nc.scalar.dma_start(wb_sb[:], wb)
 
         u_own = held.tile([NA * R, N], BF16, name="u_own")
         nc.vector.memset(u_own[:], 0.0)

@@ -33,7 +33,7 @@ def tile_llamaattentionwithlora_kernel(tc, table, w, wa, wb, offs, out):
         w_sb = held.tile([D, M], BF16, name="w_sb")
         nc.scalar.dma_start(w_sb[:], w)
         wb_sb = held.tile([NA * R, M], BF16, name="wb_sb")
-        nc.scalar.dma_start(wb_sb[:], wb)
+        nc.sync.dma_start(wb_sb[:], wb)
 
         u_own = held.tile([NA * R, N], BF16, name="u_own")
         nc.vector.memset(u_own[:], 0.0)

import concourse.mybir as mybir

BF16, F32, U16 = mybir.dt.bfloat16, mybir.dt.float32, mybir.dt.uint16

D = 128
M = 128
S = 1024
N = 1024
NA = 4
R = 32
L = N // NA
PIECE = 512
NP = N // PIECE
K = PIECE // 16

FLOPS = 2 * D * M * N + 2 * D * (NA * R) * N + 2 * R * M * N


def tile_llamaattentionwithlora_kernel(tc, table, w, wa, wb, offs, out):
    nc = tc.nc
    with (
        tc.tile_pool(name="held", bufs=1) as held,
        tc.tile_pool(name="staged", bufs=NP) as staged,
        tc.psum_pool(name="down", bufs=NP) as down,
        tc.psum_pool(name="proj", bufs=NP) as proj,
    ):
        table_sb = held.tile([D, S], BF16, name="table_sb")
        nc.sync.dma_start(table_sb[:], table)
        offsets = held.tile([128, N // 16], U16, name="offsets")
        nc.sync.dma_start(offsets[:], offs)
        wa_sb = held.tile([D, NA * R], BF16, name="wa_sb")
        nc.scalar.dma_start(wa_sb[:], wa)
        w_sb = held.tile([D, M], BF16, name="w_sb")
        nc.scalar.dma_start(w_sb[:], w)
        wb_sb = held.tile([NA * R, M], BF16, name="wb_sb")
        nc.sync.dma_start(wb_sb[:], wb)

        u_own = held.tile([NA * R, N], BF16, name="u_own")
        nc.vector.memset(u_own[:], 0.0)

        for p in range(NP):
            picked = table_sb[:].indirect(offsets[:, p * K : (p + 1) * K])
            u_ps = down.tile([NA * R, PIECE], F32, name="u_ps")
            nc.tensor.matmul(u_ps[:], wa_sb[:], picked, start=True, stop=True)
            for a in range(p * PIECE // L, (p + 1) * PIECE // L):
                own_rows = slice(a * R, (a + 1) * R)
                if a % 2 == 0:
                    nc.vector.tensor_copy(u_own[own_rows, a * L : (a + 1) * L], u_ps[own_rows, a * L - p * PIECE : (a + 1) * L - p * PIECE])
                else:
                    nc.scalar.copy(u_own[own_rows, a * L : (a + 1) * L], u_ps[own_rows, a * L - p * PIECE : (a + 1) * L - p * PIECE])

        out_ps = [proj.tile([M, PIECE], F32, name="out_ps") for p in range(NP)]
        for p in range(NP):
            picked = table_sb[:].indirect(offsets[:, p * K : (p + 1) * K])
            nc.tensor.matmul(out_ps[p][:], w_sb[:], picked, start=True, stop=False)

        for p in range(NP):
            nc.tensor.matmul(out_ps[p][:], wb_sb[:], u_own[:, p * PIECE : (p + 1) * PIECE], start=False, stop=True)
            out_sb = staged.tile([M, PIECE], F32, name="out_sb")
            if p % 2 == 0:
                nc.vector.tensor_copy(out_sb[:], out_ps[p][:])
                nc.sync.dma_start(out[:, p * PIECE : (p + 1) * PIECE], out_sb[:])
            else:
                nc.scalar.copy(out_sb[:], out_ps[p][:])
                nc.scalar.dma_start(out[:, p * PIECE : (p + 1) * PIECE], out_sb[:])
